import numpy as np
import ml_dtypes


def mxq(x, axis, fmt="e4m3"):
    dtype, down = {"e4m3": (ml_dtypes.float8_e4m3fn, 7), "e5m2": (ml_dtypes.float8_e5m2, 14)}[fmt]
    v = np.moveaxis(np.asarray(x, np.float32).astype(ml_dtypes.bfloat16).astype(np.float64), axis, -1)
    blocks = v.reshape(v.shape[:-1] + (-1, 32))
    amax = np.abs(blocks).max(-1, keepdims=True)
    byte = np.maximum(np.where(amax > 0, np.frexp(amax)[1] - 1 + 127, 0) - down, 1)
    scale = np.exp2(byte - 127.0)
    codes = (blocks / scale).astype(np.float32).astype(dtype).astype(np.float64)
    return np.moveaxis((codes * scale).reshape(v.shape), -1, axis)


WIDE = False


def mx_kscale(k):
    if not WIDE:
        return np.ones(k)
    levels = np.array([10, -10, 5, -5, 0])
    a = np.random.permutation(np.resize(levels, k // 512 * 4)).reshape(k // 512, 4)
    idx = np.arange(k)
    return np.exp2(a[idx // 512, idx % 128 // 32])


BF16 = ml_dtypes.bfloat16


def bf(x):
    return np.asarray(x, np.float32).astype(BF16)


def f64(x):
    return np.asarray(x).astype(np.float64)


B, S, H = 2, 256, 1536
M = B * S


def setup_inputs():
    s = mx_kscale(H)
    return {"x": bf(np.random.standard_normal((B, S, H)) * s),
            "plastic_weights": bf(np.random.standard_normal((H, H)) / np.sqrt(H) / s[None, :]),
            "plasticity_rate": bf(np.random.uniform(0.2, 0.4, 1)),
            "fixed_w": bf(np.random.standard_normal((H, H)) / np.sqrt(H) / s[None, :]),
            "fixed_b": bf(np.random.standard_normal(H) * 0.3),
            "hebbian_strength": bf(np.random.uniform(1.5, 2.5, 1))}


def reference(x, plastic_weights, plasticity_rate, fixed_w, fixed_b, hebbian_strength):
    xf = f64(x)
    pw = f64(plastic_weights)
    xq = mxq(xf, 2, "e4m3")
    fixed_out = (xq @ mxq(f64(fixed_w), 1, "e4m3").T) + f64(fixed_b)
    plastic_out = xq @ mxq(pw, 1, "e4m3").T
    combined = fixed_out + plastic_out
    pre = mxq(xf.reshape(M, H), 0, "e4m3")
    post = mxq(combined.reshape(M, H), 0, "e4m3")
    hebb = (pre.T @ post) / M
    plasticity_factor = f64(plasticity_rate)[0] * f64(hebbian_strength)
    new_w = pw + plasticity_factor * hebb
    w_norm = np.sqrt(np.sum(new_w ** 2))
    new_w = np.where(w_norm > 1.0, new_w / w_norm, new_w)
    return combined, new_w

@@ -1,0 +1,387 @@
+from contextlib import ExitStack
+
+import concourse.bass as bass
+import concourse.mybir as mybir
+import concourse.tile as tile
+from concourse.masks import make_identity
+
+F32 = mybir.dt.float32
+BF16 = mybir.dt.bfloat16
+U32 = mybir.dt.uint32
+U8 = mybir.dt.uint8
+I32 = mybir.dt.int32
+FP8X4 = mybir.dt.float8_e4m3fn_x4
+ALU = mybir.AluOpType
+ACT = mybir.ActivationFunctionType
+AX = mybir.AxisListType
+
+P = 128
+H = 1536
+M = 512
+KP = 512
+NG = H // KP
+NJ = M // P
+BW = 256
+NB = H // BW
+NT = H // P
+FLOPS = 3 * 2 * M * H * H
+PINNED = True
+S2_PER_ROUND = 3
+WIDTHS = (256, 256, 256, 256, 256, 256)
+FAST_LAST = 1
+NH = 6
+WQ_BUFS = 4
+T_FIRST = 2
+T_PER_ROUND = (1, 1, 1, 1, 1, 1, 1, 1, 1, 1)
+
+
+def tile_neuroplasticitylayer_kernel(
+    tc, x, plastic_weights, plasticity_rate, fixed_w, fixed_b, hebbian_strength, out_0, out_1
+):
+    nc = tc.nc
+    with ExitStack() as ctx:
+        if PINNED:
+            ctx.enter_context(tc.manual_schedule())
+        const = ctx.enter_context(tc.tile_pool(name="const", bufs=1))
+        big = ctx.enter_context(tc.tile_pool(name="big", bufs=1))
+        grp = ctx.enter_context(tc.tile_pool(name="grp", bufs=8))
+        wq = ctx.enter_context(tc.tile_pool(name="wq", bufs=WQ_BUFS))
+        cb = ctx.enter_context(tc.tile_pool(name="cb", bufs=3))
+        psum = ctx.enter_context(tc.psum_pool(name="psum", bufs=1))
+
+        x_v = x.flatten_outer_dims().rearrange("(p j) h -> p j h", j=NJ)
+        out0_v = out_0.flatten_outer_dims().rearrange("(p j) o -> p j o", j=NJ)
+        w_v = [
+            plastic_weights.rearrange("(t p) h -> p t h", p=P),
+            fixed_w.rearrange("(t p) h -> p t h", p=P),
+        ]
+        out1_v = out_1.rearrange("(t p) o -> p t o", p=P)
+
+        x_sb = big.tile([P, NJ, H], BF16, name="x_sb")
+        pw_sb = big.tile([P, NT, H], BF16, name="pw_sb")
+        fw_sb = big.tile([P, NT, H], BF16, name="fw_sb")
+        w_sb = [pw_sb, fw_sb]
+        t_sb = big.tile([P, NT, H], F32, name="t_sb")
+        xc = big.tile([P, NG, M], U32, name="xc", align_bytes=64)
+        xs = big.tile([P, NG, M], U8, name="xs", align_bytes=64)
+        prec = big.tile([P, H], U32, name="prec", align_bytes=64)
+        pres = big.tile([P, H], U8, name="pres", align_bytes=64)
+
+        ident = const.tile([P, P], F32, name="ident")
+        ones_bf = const.tile([P, P], BF16, name="ones_bf")
+        ones_f = const.tile([P, P], F32, name="ones_f")
+        brow = cb.tile([P, 2048], BF16, name="brow", tag="comb")
+        bias_bc = const.tile([P, H], BF16, name="bias_bc")
+        rate = const.tile([P, 1], BF16, name="rate")
+        stren = const.tile([P, 1], BF16, name="stren")
+        cfac = const.tile([P, 1], F32, name="cfac")
+        warm = const.tile([P, 1], F32, name="warm")
+        NSQ = 40
+        sq = const.tile([P, NSQ], F32, name="sq")
+        tot = const.tile([P, 1], F32, name="tot")
+        nrm = const.tile([P, 1], F32, name="nrm")
+        inv = const.tile([P, 1], F32, name="inv")
+
+        nc.vector.memset(brow[:].bitcast(I32), 0)
+        nc.vector.memset(ones_bf[:], 1.0)
+        nc.vector.memset(ones_f[:], 1.0)
+        make_identity(nc, ident[:])
+        nc.sync.dma_start(out=brow[0:1, 0:H], in_=fixed_b.unsqueeze(0))
+        nc.scalar.dma_start(out=rate[:], in_=plasticity_rate.partition_broadcast(P))
+        nc.scalar.dma_start(out=stren[:], in_=hebbian_strength.partition_broadcast(P))
+        nc.scalar.activation(out=warm[:], in_=ones_f[:, 0:1], func=ACT.Sqrt)
+
+        blocks = []
+        c0 = 0
+        for wd in WIDTHS:
+            blocks.append((c0, wd))
+            c0 += wd
+        assert c0 == H
+        units = []
+        for b, (c0, wd) in enumerate(blocks):
+            if wd == 256:
+                units.append((b, (0,)))
+                units.append((b, (1,)))
+            else:
+                units.append((b, (0, 1)))
+        NU = len(units)
+        block_units = [[n for n in range(NU) if units[n][0] == b] for b in range(len(blocks))]
+
+        def load_x(h):
+            nc.sync.dma_start(out=x_sb[:, 2 * h : 2 * h + 2, :], in_=x_v[:, 2 * h : 2 * h + 2, :])
+
+        def load_w(n):
+            b, ws_ = units[n]
+            c0, wd = blocks[b]
+            ts = slice(c0 // P, (c0 + wd) // P)
+            for w in ws_:
+                nc.sync.dma_start(out=w_sb[w][:, ts, :], in_=w_v[w][:, ts, :])
+
+        load_x(0)
+        load_w(0)
+        load_w(1)
+        load_x(1)
+        for n in range(2, NU):
+            load_w(n)
+
+        def bias_everywhere():
+            for i in range(3):
+                bb = next_h([P, 512])
+                cs = slice(i * 512, (i + 1) * 512)
+                nc.tensor.matmul(out=bb[:], lhsT=ones_bf[:], rhs=brow[:, cs], start=True, stop=True)
+                nc.scalar.copy(out=bias_bc[:, cs], in_=bb[:])
+
+        state = {"h": 0, "sq": 0, "a": 0}
+        wcodes = {}
+        acc = {}
+        posts = {}
+        combs = {}
+        s2_ready = []
+        to_square = []
+        v_later = []
+        post_q = []
+
+        def next_h(shape):
+            i = state["h"] % NH
+            state["h"] += 1
+            return psum.tile(shape, F32, name="hb", tag="H%d" % i)
+
+        def transpose_bank(srcs):
+            bank = next_h([P, 2, 2, P])
+            for i in range(4):
+                nc.tensor.transpose(out=bank[:, i // 2, i % 2, :], in_=srcs[i].bitcast(F32), identity=ident[:])
+            return bank
+
+        def exit_bank(bank):
+            g_t = grp.tile([P, 1024], BF16, name="g_t", tag="grp", align_bytes=64)
+            nc.scalar.copy(
+                out=g_t[:].bitcast(F32).rearrange("p (a r u) -> p a r u", a=2, u=2),
+                in_=bank[:].rearrange("p a u r -> p a r u"),
+            )
+            return g_t
+
+        def t_rows(rows, codes, planes):
+            banks = [
+                transpose_bank([row[:, g * KP + u * 256 : g * KP + (u + 1) * 256] for row in rows for u in range(2)])
+                for g in range(NG)
+            ]
+            tiles = [exit_bank(bank) for bank in banks]
+            return [
+                lambda g=g: nc.vector.quantize_mx(out=codes[g].bitcast(FP8X4), scales=planes[g], in_=tiles[g][:])
+                for g in range(NG)
+            ]
+
+        def t_x(h):
+            hs = slice(h * 256, (h + 1) * 256)
+            return t_rows(
+                [x_sb[:, 2 * h + a, :] for a in range(2)],
+                [xc[:, g, hs] for g in range(NG)],
+                [xs[:, g, hs] for g in range(NG)],
+            )
+
+        def t_w(n):
+            b, ws_ = units[n]
+            t0 = blocks[b][0] // P
+            rows = [w_sb[ws_[0]][:, t0 + a, :] for a in range(2)] if len(ws_) == 1 else [w_sb[w][:, t0, :] for w in ws_]
+            wc = wq.tile([P, NG, BW], U32, name="wc", tag="wc", align_bytes=64)
+            ws = wq.tile([P, NG, BW], U8, name="ws", tag="ws", align_bytes=64)
+            wcodes[n] = (wc, ws)
+            return t_rows(rows, [wc[:, g, :] for g in range(NG)], [ws[:, g, :] for g in range(NG)])
+
+        def pre_chunk(c):
+            g_t = grp.tile([P, 1024], BF16, name="g_t", tag="grp", align_bytes=64)
+            cs = slice(c * 256, (c + 1) * 256)
+            nc.gpsimd.tensor_scalar(
+                out=g_t[:].rearrange("p (o j) -> p o j", j=NJ),
+                in0=x_sb[:, :, cs].rearrange("p j o -> p o j"),
+                scalar1=1.0,
+                scalar2=0.0,
+                op0=ALU.mult,
+                op1=ALU.add,
+            )
+            return lambda: nc.vector.quantize_mx(out=prec[:, cs].bitcast(FP8X4), scales=pres[:, cs], in_=g_t[:])
+
+        def s1(b, j, a_t):
+            c0, wd = blocks[b]
+            sl = slice(j * P, (j + 1) * P)
+            passes = [(n, w, g) for n in block_units[b] for w in units[n][1] for g in range(NG)]
+            for i, (n, w, g) in enumerate(passes):
+                wc, ws = wcodes[n]
+                cs = slice(0, wd) if len(units[n][1]) == 1 else slice(w * wd, (w + 1) * wd)
+                nc.tensor.matmul_mx(
+                    out=a_t,
+                    lhsT=xc[:, g, sl].bitcast(FP8X4),
+                    lhsT_scale=xs[:, g, sl],
+                    rhs=wc[:, g, cs].bitcast(FP8X4),
+                    rhs_scale=ws[:, g, cs],
+                    start=(i == 0),
+                    stop=(i == len(passes) - 1),
+                )
+
+        def close_rows(b, js, a_t):
+            c0, wd = blocks[b]
+            if b not in combs:
+                combs[b] = cb.tile([P, NJ, wd], F32, name="comb", tag="comb")
+            nc.vector.tensor_tensor(
+                out=combs[b][:, js[0] : js[-1] + 1, :],
+                in0=a_t[:],
+                in1=bias_bc[:, c0 : c0 + wd].unsqueeze(1).to_broadcast([P, len(js), wd]),
+                op=ALU.add,
+            )
+
+        def close_block(b, fast):
+            c0, wd = blocks[b]
+            comb = combs[b]
+            nc.sync.dma_start(out=out0_v[:, :, c0 : c0 + wd], in_=comb[:])
+            cg = cb.tile([P, wd * NJ], BF16, name="cg", tag="cg", align_bytes=64)
+            if fast:
+                nc.vector.tensor_copy(
+                    out=cg[:].rearrange("p (o j) -> p o j", j=NJ), in_=comb[:].rearrange("p j o -> p o j")
+                )
+            else:
+                nc.gpsimd.tensor_scalar(
+                    out=cg[:].rearrange("p (o j) -> p o j", j=NJ),
+                    in0=comb[:].rearrange("p j o -> p o j"),
+                    scalar1=1.0,
+                    scalar2=0.0,
+                    op0=ALU.mult,
+                    op1=ALU.add,
+                )
+
+            def quant():
+                pc = cb.tile([P, wd], U32, name="pc", tag="pc", align_bytes=64)
+                ps = cb.tile([P, wd], U8, name="ps", tag="ps", align_bytes=64)
+                nc.vector.quantize_mx(out=pc[:].bitcast(FP8X4), scales=ps[:], in_=cg[:])
+                posts[b] = (pc, ps)
+                per = 512 // wd
+                for k in range(NT // per):
+                    s2_ready.append((b, k * per, per))
+
+            return quant
+
+        def s2_pe(b, t0, per):
+            pc, ps = posts[b]
+            hb = next_h([P, per, blocks[b][1]])
+            for i in range(per):
+                ts = slice((t0 + i) * P, (t0 + i + 1) * P)
+                nc.tensor.matmul_mx(
+                    out=hb[:, i, :],
+                    lhsT=prec[:, ts].bitcast(FP8X4),
+                    lhsT_scale=pres[:, ts],
+                    rhs=pc[:].bitcast(FP8X4),
+                    rhs_scale=ps[:],
+                    start=True,
+                    stop=True,
+                )
+            return hb
+
+        def s2_out(b, t0, per, hb):
+            c0, wd = blocks[b]
+            nc.vector.scalar_tensor_tensor(
+                out=t_sb[:, t0 : t0 + per, c0 : c0 + wd],
+                in0=hb[:],
+                scalar=cfac[:, 0:1],
+                in1=pw_sb[:, t0 : t0 + per, c0 : c0 + wd],
+                op0=ALU.mult,
+                op1=ALU.add,
+            )
+            to_square.append((b, t0, per))
+
+        def squares(group):
+            while to_square:
+                b, t0, per = to_square.pop(0)
+                n = per
+                while n < group * per and to_square and to_square[0] == (b, t0 + n, per):
+                    to_square.pop(0)
+                    n += per
+                c0, wd = blocks[b]
+                i = state["sq"]
+                state["sq"] += 1
+                nc.scalar.activation(
+                    out=x_sb[:, 0, 0 : n * wd].rearrange("p (a o) -> p a o", o=wd),
+                    in_=t_sb[:, t0 : t0 + n, c0 : c0 + wd],
+                    func=ACT.Square,
+                    accum_out=sq[:, i : i + 1],
+                )
+
+        def s2_run(count):
+            jobs = []
+            for i in range(min(count, len(s2_ready))):
+                job = s2_ready.pop(0)
+                jobs.append(job + (s2_pe(*job),))
+            return jobs
+
+        def drain(queue):
+            while queue:
+                queue.pop(0)()
+
+        rounds = []
+        for b, (c0, wd) in enumerate(blocks):
+            if wd == 256:
+                rounds.append((b, (0, 1)))
+                rounds.append((b, (2, 3)))
+            else:
+                rounds.append((b, (0, 1, 2, 3)))
+        tq = list(range(NU))
+        for q in t_x(0):
+            q()
+        bias_everywhere()
+        for i in range(T_FIRST):
+            for q in t_w(tq.pop(0)):
+                q()
+        for q in t_x(1):
+            q()
+        pre_q = []
+        for r, (b, js) in enumerate(rounds):
+            quants = []
+            for i in range(T_PER_ROUND[r] if r < len(T_PER_ROUND) else 0):
+                if tq:
+                    quants = quants + t_w(tq.pop(0))
+            squares(3)
+            drain(v_later)
+            half = len(js) // 2
+            a_t = psum.tile([P, len(js), blocks[b][1]], F32, name="a_t", tag="A%d" % (r % 2))
+            for j in js[:half]:
+                s1(b, j, a_t[:, j - js[0], :])
+            for q in quants[:2]:
+                q()
+            drain(pre_q)
+            jobs = s2_run(S2_PER_ROUND)
+            for q in quants[2:]:
+                q()
+            for job in jobs:
+                s2_out(*job)
+            drain(post_q)
+            for j in js[half:]:
+                s1(b, j, a_t[:, j - js[0], :])
+            v_later.append(lambda b=b, js=js, a_t=a_t: close_rows(b, js, a_t))
+            if r == 0:
+                nc.vector.scalar_tensor_tensor(
+                    out=cfac[:], in0=rate[:], scalar=1.0 / M, in1=stren[:], op0=ALU.mult, op1=ALU.mult
+                )
+            if r < 3:
+                pre_q.append(pre_chunk(2 * r))
+                pre_q.append(pre_chunk(2 * r + 1))
+            if js[-1] == NJ - 1:
+                v_later.append(lambda b=b: post_q.append(close_block(b, b >= len(blocks) - FAST_LAST)))
+        while v_later or post_q or s2_ready or to_square:
+            drain(v_later)
+            drain(post_q)
+            for job in s2_run(2):
+                s2_out(*job)
+            squares(2)
+
+        nsq = state["sq"]
+        assert nsq <= NSQ
+        tp = psum.tile([P, NSQ], F32, name="tp", tag="A0")
+        nc.tensor.matmul(out=tp[:, 0:nsq], lhsT=ones_f[:], rhs=sq[:, 0:nsq], start=True, stop=True)
+        nc.vector.tensor_reduce(out=tot[:], in_=tp[:, 0:nsq], axis=AX.X, op=ALU.add)
+        nc.vector.tensor_scalar_max(out=tot[:], in0=tot[:], scalar1=1.0)
+        nc.scalar.activation(out=nrm[:], in_=tot[:], func=ACT.Sqrt)
+        nc.vector.reciprocal(out=inv[:], in_=nrm[:])
+        for it in range(NT):
+            if it % 3 == 1:
+                nc.scalar.activation(out=t_sb[:, it, :], in_=t_sb[:, it, :], func=ACT.Copy, scale=inv[:, 0:1])
+            else:
+                nc.vector.tensor_scalar_mul(out=t_sb[:, it, :], in0=t_sb[:, it, :], scalar1=inv[:, 0:1])
+            nc.sync.dma_start(out=out1_v[:, it, :], in_=t_sb[:, it, :])

@@ -30,8 +30,8 @@ S2_PER_ROUND = 3
 WIDTHS = (256, 256, 256, 256, 256, 256)
 FAST_LAST = 1
 NH = 6
-WQ_BUFS = 4
-T_FIRST = 2
+WQ_BUFS = 5
+T_FIRST = 3
 T_PER_ROUND = (1, 1, 1, 1, 1, 1, 1, 1, 1, 1)
 
 
@@ -191,13 +191,9 @@ def tile_neuroplasticitylayer_kernel(
         def pre_chunk(c):
             g_t = grp.tile([P, 1024], BF16, name="g_t", tag="grp", align_bytes=64)
             cs = slice(c * 256, (c + 1) * 256)
-            nc.gpsimd.tensor_scalar(
-                out=g_t[:].rearrange("p (o j) -> p o j", j=NJ),
-                in0=x_sb[:, :, cs].rearrange("p j o -> p o j"),
-                scalar1=1.0,
-                scalar2=0.0,
-                op0=ALU.mult,
-                op1=ALU.add,
+            nc.vector.tensor_copy(
+                out=g_t[:].rearrange("p (c i t) -> p c t i", i=4, t=4),
+                in_=x_sb[:, :, cs].rearrange("p t (c i) -> p c t i", i=4),
             )
             return lambda: nc.vector.quantize_mx(out=prec[:, cs].bitcast(FP8X4), scales=pres[:, cs], in_=g_t[:])
 
@@ -326,34 +322,32 @@ def tile_neuroplasticitylayer_kernel(
         for q in t_x(0):
             q()
         bias_everywhere()
-        for i in range(T_FIRST):
+        for i in range(2):
             for q in t_w(tq.pop(0)):
                 q()
-        for q in t_x(1):
-            q()
+        q_prev = t_x(1)
         pre_q = []
+        for i in range(T_FIRST - 2):
+            q_next = t_w(tq.pop(0))
+            drain(q_prev)
+            q_prev = q_next
         for r, (b, js) in enumerate(rounds):
-            quants = []
-            for i in range(T_PER_ROUND[r] if r < len(T_PER_ROUND) else 0):
-                if tq:
-                    quants = quants + t_w(tq.pop(0))
-            squares(3)
-            drain(v_later)
             half = len(js) // 2
+            jobs = s2_run(S2_PER_ROUND)
             a_t = psum.tile([P, len(js), blocks[b][1]], F32, name="a_t", tag="A%d" % (r % 2))
             for j in js[:half]:
                 s1(b, j, a_t[:, j - js[0], :])
-            for q in quants[:2]:
-                q()
+            squares(3)
+            q_next = t_w(tq.pop(0)) if tq else []
+            for j in js[half:]:
+                s1(b, j, a_t[:, j - js[0], :])
+            drain(q_prev)
+            q_prev = q_next
             drain(pre_q)
-            jobs = s2_run(S2_PER_ROUND)
-            for q in quants[2:]:
-                q()
+            drain(v_later)
             for job in jobs:
                 s2_out(*job)
             drain(post_q)
-            for j in js[half:]:
-                s1(b, j, a_t[:, j - js[0], :])
             v_later.append(lambda b=b, js=js, a_t=a_t: close_rows(b, js, a_t))
             if r == 0:
                 nc.vector.scalar_tensor_tensor(

@@ -82,11 +82,10 @@ def tile_neuroplasticitylayer_kernel(
         nrm = const.tile([P, 1], F32, name="nrm")
         inv = const.tile([P, 1], F32, name="inv")
 
-        nc.vector.memset(brow[:].bitcast(I32), 0)
+        nc.vector.memset(brow[:, 0:H].bitcast(I32), 0)
         nc.vector.memset(ones_bf[:], 1.0)
         nc.vector.memset(ones_f[:], 1.0)
         make_identity(nc, ident[:])
-        nc.sync.dma_start(out=brow[0:1, 0:H], in_=fixed_b.unsqueeze(0))
         nc.scalar.dma_start(out=rate[:], in_=plasticity_rate.partition_broadcast(P))
         nc.scalar.dma_start(out=stren[:], in_=hebbian_strength.partition_broadcast(P))
         nc.scalar.activation(out=warm[:], in_=ones_f[:, 0:1], func=ACT.Sqrt)
@@ -118,9 +117,10 @@ def tile_neuroplasticitylayer_kernel(
                 nc.sync.dma_start(out=w_sb[w][:, ts, :], in_=w_v[w][:, ts, :])
 
         load_x(0)
+        nc.sync.dma_start(out=brow[0:1, 0:H], in_=fixed_b.unsqueeze(0))
+        load_x(1)
         load_w(0)
         load_w(1)
-        load_x(1)
         for n in range(2, NU):
             load_w(n)
 
@@ -152,41 +152,44 @@ def tile_neuroplasticitylayer_kernel(
                 nc.tensor.transpose(out=bank[:, i // 2, i % 2, :], in_=srcs[i].bitcast(F32), identity=ident[:])
             return bank
 
-        def exit_bank(bank):
+        def exit_bank(bank, on_vector):
             g_t = grp.tile([P, 1024], BF16, name="g_t", tag="grp", align_bytes=64)
-            nc.scalar.copy(
-                out=g_t[:].bitcast(F32).rearrange("p (a r u) -> p a r u", a=2, u=2),
-                in_=bank[:].rearrange("p a u r -> p a r u"),
-            )
+            dst = g_t[:].bitcast(F32).rearrange("p (a r u) -> p a r u", a=2, u=2)
+            src = bank[:].rearrange("p a u r -> p a r u")
+            if on_vector:
+                nc.vector.tensor_copy(out=dst, in_=src)
+            else:
+                nc.scalar.copy(out=dst, in_=src)
             return g_t
 
-        def t_rows(rows, codes, planes):
+        def t_rows(rows, codes, planes, on_vector=()):
             banks = [
                 transpose_bank([row[:, g * KP + u * 256 : g * KP + (u + 1) * 256] for row in rows for u in range(2)])
                 for g in range(NG)
             ]
-            tiles = [exit_bank(bank) for bank in banks]
+            tiles = [exit_bank(bank, g in on_vector) for g, bank in enumerate(banks)]
             return [
                 lambda g=g: nc.vector.quantize_mx(out=codes[g].bitcast(FP8X4), scales=planes[g], in_=tiles[g][:])
                 for g in range(NG)
             ]
 
-        def t_x(h):
+        def t_x(h, on_vector):
             hs = slice(h * 256, (h + 1) * 256)
             return t_rows(
                 [x_sb[:, 2 * h + a, :] for a in range(2)],
                 [xc[:, g, hs] for g in range(NG)],
                 [xs[:, g, hs] for g in range(NG)],
+                on_vector,
             )
 
-        def t_w(n):
+        def t_w(n, on_vector=()):
             b, ws_ = units[n]
             t0 = blocks[b][0] // P
             rows = [w_sb[ws_[0]][:, t0 + a, :] for a in range(2)] if len(ws_) == 1 else [w_sb[w][:, t0, :] for w in ws_]
             wc = wq.tile([P, NG, BW], U32, name="wc", tag="wc", align_bytes=64)
             ws = wq.tile([P, NG, BW], U8, name="ws", tag="ws", align_bytes=64)
             wcodes[n] = (wc, ws)
-            return t_rows(rows, [wc[:, g, :] for g in range(NG)], [ws[:, g, :] for g in range(NG)])
+            return t_rows(rows, [wc[:, g, :] for g in range(NG)], [ws[:, g, :] for g in range(NG)], on_vector)
 
         def pre_chunk(c):
             g_t = grp.tile([P, 1024], BF16, name="g_t", tag="grp", align_bytes=64)
@@ -319,18 +322,21 @@ def tile_neuroplasticitylayer_kernel(
             else:
                 rounds.append((b, (0, 1, 2, 3)))
         tq = list(range(NU))
-        for q in t_x(0):
-            q()
-        bias_everywhere()
-        for i in range(2):
-            for q in t_w(tq.pop(0)):
-                q()
-        q_prev = t_x(1)
+        drain(t_x(0, (1,)))
         pre_q = []
-        for i in range(T_FIRST - 2):
-            q_next = t_w(tq.pop(0))
-            drain(q_prev)
-            q_prev = q_next
+        qx1 = t_x(1, ())
+        pre_q.append(pre_chunk(0))
+        drain(qx1)
+        qw0 = t_w(tq.pop(0))
+        pre_q.append(pre_chunk(1))
+        drain(pre_q)
+        drain(qw0)
+        qw1 = t_w(tq.pop(0))
+        pre_q.append(pre_chunk(2))
+        drain(pre_q)
+        drain(qw1)
+        bias_everywhere()
+        q_prev = t_w(tq.pop(0))
         for r, (b, js) in enumerate(rounds):
             half = len(js) // 2
             jobs = s2_run(S2_PER_ROUND)
@@ -354,8 +360,7 @@ def tile_neuroplasticitylayer_kernel(
                     out=cfac[:], in0=rate[:], scalar=1.0 / M, in1=stren[:], op0=ALU.mult, op1=ALU.mult
                 )
             if r < 3:
-                pre_q.append(pre_chunk(2 * r))
-                pre_q.append(pre_chunk(2 * r + 1))
+                pre_q.append(pre_chunk(3 + r))
             if js[-1] == NJ - 1:
                 v_later.append(lambda b=b: post_q.append(close_block(b, b >= len(blocks) - FAST_LAST)))
         while v_later or post_q or s2_ready or to_square:

@@ -27,9 +27,12 @@ NT = H // P
 FLOPS = 3 * 2 * M * H * H
 PINNED = True
 S2_PER_ROUND = 3
-WIDTHS = (256, 256, 256, 256, 256, 256)
-FAST_LAST = 1
+WIDTHS = (256, 256, 256, 256, 256, 128, 128)
+FAST = (0, 6)
 NH = 6
+ROW = H + 32
+LAST_ON_VECTOR = (0,)
+PRE_ON_SCALAR = (4, 5)
 WQ_BUFS = 5
 T_FIRST = 3
 T_PER_ROUND = (1, 1, 1, 1, 1, 1, 1, 1, 1, 1)
@@ -68,26 +71,23 @@ def tile_neuroplasticitylayer_kernel(
         pres = big.tile([P, H], U8, name="pres", align_bytes=64)
 
         ident = const.tile([P, P], F32, name="ident")
-        ones_bf = const.tile([P, P], BF16, name="ones_bf")
+        ones_bf = const.tile([P, 512], BF16, name="ones_bf")
         ones_f = const.tile([P, P], F32, name="ones_f")
         brow = cb.tile([P, 2048], BF16, name="brow", tag="comb")
-        bias_bc = const.tile([P, H], BF16, name="bias_bc")
-        rate = const.tile([P, 1], BF16, name="rate")
-        stren = const.tile([P, 1], BF16, name="stren")
+        bias_bc = const.tile([P, ROW], BF16, name="bias_bc")
         cfac = const.tile([P, 1], F32, name="cfac")
         warm = const.tile([P, 1], F32, name="warm")
         NSQ = 40
         sq = const.tile([P, NSQ], F32, name="sq")
         tot = const.tile([P, 1], F32, name="tot")
+        early = const.tile([P, 1], F32, name="early")
         nrm = const.tile([P, 1], F32, name="nrm")
         inv = const.tile([P, 1], F32, name="inv")
 
-        nc.vector.memset(brow[:, 0:H].bitcast(I32), 0)
+        nc.vector.memset(brow[:, 0:ROW].bitcast(I32), 0)
         nc.vector.memset(ones_bf[:], 1.0)
         nc.vector.memset(ones_f[:], 1.0)
         make_identity(nc, ident[:])
-        nc.scalar.dma_start(out=rate[:], in_=plasticity_rate.partition_broadcast(P))
-        nc.scalar.dma_start(out=stren[:], in_=hebbian_strength.partition_broadcast(P))
         nc.scalar.activation(out=warm[:], in_=ones_f[:, 0:1], func=ACT.Sqrt)
 
         blocks = []
@@ -117,7 +117,9 @@ def tile_neuroplasticitylayer_kernel(
                 nc.sync.dma_start(out=w_sb[w][:, ts, :], in_=w_v[w][:, ts, :])
 
         load_x(0)
-        nc.sync.dma_start(out=brow[0:1, 0:H], in_=fixed_b.unsqueeze(0))
+        nc.scalar.dma_start(out=brow[0:1, 0:H], in_=fixed_b.unsqueeze(0))
+        nc.scalar.dma_start(out=brow[0:1, H : H + 1], in_=plasticity_rate.unsqueeze(0))
+        nc.scalar.dma_start(out=brow[0:1, H + 16 : H + 17], in_=hebbian_strength.unsqueeze(0))
         load_x(1)
         load_w(0)
         load_w(1)
@@ -125,10 +127,10 @@ def tile_neuroplasticitylayer_kernel(
             load_w(n)
 
         def bias_everywhere():
-            for i in range(3):
-                bb = next_h([P, 512])
-                cs = slice(i * 512, (i + 1) * 512)
-                nc.tensor.matmul(out=bb[:], lhsT=ones_bf[:], rhs=brow[:, cs], start=True, stop=True)
+            for i in range(4):
+                bb = next_h([P, ROW // 4])
+                cs = slice(i * ROW // 4, (i + 1) * ROW // 4)
+                nc.tensor.matmul(out=bb[:], lhsT=ones_bf[:, 0:P], rhs=brow[:, cs], start=True, stop=True)
                 nc.scalar.copy(out=bias_bc[:, cs], in_=bb[:])
 
         state = {"h": 0, "sq": 0, "a": 0}
@@ -194,10 +196,12 @@ def tile_neuroplasticitylayer_kernel(
         def pre_chunk(c):
             g_t = grp.tile([P, 1024], BF16, name="g_t", tag="grp", align_bytes=64)
             cs = slice(c * 256, (c + 1) * 256)
-            nc.vector.tensor_copy(
-                out=g_t[:].rearrange("p (c i t) -> p c t i", i=4, t=4),
-                in_=x_sb[:, :, cs].rearrange("p t (c i) -> p c t i", i=4),
-            )
+            pre_dst = g_t[:].rearrange("p (c i t) -> p c t i", i=4, t=4)
+            pre_src = x_sb[:, :, cs].rearrange("p t (c i) -> p c t i", i=4)
+            if c in PRE_ON_SCALAR:
+                nc.scalar.copy(out=pre_dst, in_=pre_src)
+            else:
+                nc.vector.tensor_copy(out=pre_dst, in_=pre_src)
             return lambda: nc.vector.quantize_mx(out=prec[:, cs].bitcast(FP8X4), scales=pres[:, cs], in_=g_t[:])
 
         def s1(b, j, a_t):
@@ -286,7 +290,7 @@ def tile_neuroplasticitylayer_kernel(
             )
             to_square.append((b, t0, per))
 
-        def squares(group):
+        def squares(group, on_vector=False):
             while to_square:
                 b, t0, per = to_square.pop(0)
                 n = per
@@ -296,6 +300,18 @@ def tile_neuroplasticitylayer_kernel(
                 c0, wd = blocks[b]
                 i = state["sq"]
                 state["sq"] += 1
+                if on_vector:
+                    t_v = t_sb[:, t0 : t0 + n, c0 : c0 + wd]
+                    nc.vector.scalar_tensor_tensor(
+                        out=fw_sb[:, 0:2, :].bitcast(F32)[:, 0, 0 : n * wd].rearrange("p (a o) -> p a o", o=wd),
+                        in0=t_v,
+                        scalar=1.0,
+                        in1=t_v,
+                        op0=ALU.mult,
+                        op1=ALU.mult,
+                        accum_out=sq[:, i : i + 1],
+                    )
+                    continue
                 nc.scalar.activation(
                     out=x_sb[:, 0, 0 : n * wd].rearrange("p (a o) -> p a o", o=wd),
                     in_=t_sb[:, t0 : t0 + n, c0 : c0 + wd],
@@ -357,30 +373,46 @@ def tile_neuroplasticitylayer_kernel(
             v_later.append(lambda b=b, js=js, a_t=a_t: close_rows(b, js, a_t))
             if r == 0:
                 nc.vector.scalar_tensor_tensor(
-                    out=cfac[:], in0=rate[:], scalar=1.0 / M, in1=stren[:], op0=ALU.mult, op1=ALU.mult
+                    out=cfac[:],
+                    in0=bias_bc[:, H : H + 1],
+                    scalar=1.0 / M,
+                    in1=bias_bc[:, H + 16 : H + 17],
+                    op0=ALU.mult, op1=ALU.mult
                 )
             if r < 3:
                 pre_q.append(pre_chunk(3 + r))
             if js[-1] == NJ - 1:
-                v_later.append(lambda b=b: post_q.append(close_block(b, b >= len(blocks) - FAST_LAST)))
-        while v_later or post_q or s2_ready or to_square:
-            drain(v_later)
-            drain(post_q)
-            for job in s2_run(2):
+                v_later.append(lambda b=b: post_q.append(close_block(b, b in FAST)))
+        nearly = state["sq"]
+        backlog = s2_run(len(s2_ready))
+        squares(3)
+        drain(v_later)
+        for job in backlog[:1]:
+            s2_out(*job)
+        squares(1)
+        drain(post_q)
+        for job in backlog[1:]:
+            s2_out(*job)
+            squares(1)
+        nc.vector.tensor_reduce(out=early[:], in_=sq[:, 0:nearly], axis=AX.X, op=ALU.add)
+        while s2_ready:
+            for job in s2_run(1):
                 s2_out(*job)
-            squares(2)
+            squares(1, on_vector=len(s2_ready) in LAST_ON_VECTOR)
 
         nsq = state["sq"]
         assert nsq <= NSQ
-        tp = psum.tile([P, NSQ], F32, name="tp", tag="A0")
-        nc.tensor.matmul(out=tp[:, 0:nsq], lhsT=ones_f[:], rhs=sq[:, 0:nsq], start=True, stop=True)
-        nc.vector.tensor_reduce(out=tot[:], in_=tp[:, 0:nsq], axis=AX.X, op=ALU.add)
-        nc.vector.tensor_scalar_max(out=tot[:], in0=tot[:], scalar1=1.0)
+        tp = psum.tile([P, 1], F32, name="tp", tag="A0")
+        parts = [early[:]] + [sq[:, i : i + 1] for i in range(nearly, nsq)]
+        for i, part in enumerate(parts):
+            nc.tensor.matmul(out=tp[:], lhsT=ones_f[:], rhs=part, start=(i == 0), stop=(i == len(parts) - 1))
+        nc.vector.tensor_scalar_max(out=tot[:], in0=tp[:], scalar1=1.0)
         nc.scalar.activation(out=nrm[:], in_=tot[:], func=ACT.Sqrt)
         nc.vector.reciprocal(out=inv[:], in_=nrm[:])
-        for it in range(NT):
-            if it % 3 == 1:
-                nc.scalar.activation(out=t_sb[:, it, :], in_=t_sb[:, it, :], func=ACT.Copy, scale=inv[:, 0:1])
+        pieces = [(0, 0, 512), (0, 512, H)] + [(it, 0, H) for it in range(1, NT)]
+        for i, (it, lo, hi) in enumerate(pieces):
+            if i % 3 == 1:
+                nc.scalar.activation(out=t_sb[:, it, lo:hi], in_=t_sb[:, it, lo:hi], func=ACT.Copy, scale=inv[:, 0:1])
             else:
-                nc.vector.tensor_scalar_mul(out=t_sb[:, it, :], in0=t_sb[:, it, :], scalar1=inv[:, 0:1])
-            nc.sync.dma_start(out=out1_v[:, it, :], in_=t_sb[:, it, :])
+                nc.vector.tensor_scalar_mul(out=t_sb[:, it, lo:hi], in0=t_sb[:, it, lo:hi], scalar1=inv[:, 0:1])
+            nc.sync.dma_start(out=out1_v[:, it, lo:hi], in_=t_sb[:, it, lo:hi])

@@ -32,7 +32,7 @@ FAST = (0, 6)
 NH = 6
 ROW = H + 32
 LAST_ON_VECTOR = (0,)
-PRE_ON_SCALAR = (4, 5)
+PRE_ON_SCALAR = (5,)
 WQ_BUFS = 5
 T_FIRST = 3
 T_PER_ROUND = (1, 1, 1, 1, 1, 1, 1, 1, 1, 1)
@@ -147,6 +147,11 @@ def tile_neuroplasticitylayer_kernel(
             i = state["h"] % NH
             state["h"] += 1
             return psum.tile(shape, F32, name="hb", tag="H%d" % i)
+
+        def warm_up(n):
+            junk = psum.tile([P, 512], F32, name="a_t", tag="A1")
+            for i in range(n):
+                nc.tensor.matmul(out=junk[:], lhsT=ones_bf[:, 0:P], rhs=ones_bf[:], start=True, stop=True)
 
         def transpose_bank(srcs):
             bank = next_h([P, 2, 2, P])
@@ -313,7 +318,7 @@ def tile_neuroplasticitylayer_kernel(
                     )
                     continue
                 nc.scalar.activation(
-                    out=x_sb[:, 0, 0 : n * wd].rearrange("p (a o) -> p a o", o=wd),
+                    out=x_sb[:, i % 2, 0 : n * wd].rearrange("p (a o) -> p a o", o=wd),
                     in_=t_sb[:, t0 : t0 + n, c0 : c0 + wd],
                     func=ACT.Square,
                     accum_out=sq[:, i : i + 1],
@@ -338,12 +343,16 @@ def tile_neuroplasticitylayer_kernel(
             else:
                 rounds.append((b, (0, 1, 2, 3)))
         tq = list(range(NU))
+        warm_up(5)
         drain(t_x(0, (1,)))
+        warm_up(1)
         pre_q = []
         qx1 = t_x(1, ())
+        warm_up(2)
         pre_q.append(pre_chunk(0))
         drain(qx1)
         qw0 = t_w(tq.pop(0))
+        warm_up(2)
         pre_q.append(pre_chunk(1))
         drain(pre_q)
         drain(qw0)
@@ -387,6 +396,7 @@ def tile_neuroplasticitylayer_kernel(
         backlog = s2_run(len(s2_ready))
         squares(3)
         drain(v_later)
+        nc.vector.tensor_reduce(out=early[:], in_=sq[:, 0:nearly], axis=AX.X, op=ALU.add)
         for job in backlog[:1]:
             s2_out(*job)
         squares(1)
@@ -394,7 +404,6 @@ def tile_neuroplasticitylayer_kernel(
         for job in backlog[1:]:
             s2_out(*job)
             squares(1)
-        nc.vector.tensor_reduce(out=early[:], in_=sq[:, 0:nearly], axis=AX.X, op=ALU.add)
         while s2_ready:
             for job in s2_run(1):
                 s2_out(*job)

@@ -31,7 +31,7 @@ WIDTHS = (256, 256, 256, 256, 256, 128, 128)
 FAST = (0, 6)
 NH = 6
 ROW = H + 32
-LAST_ON_VECTOR = (0,)
+LAST_ON_VECTOR = ()
 PRE_ON_SCALAR = (5,)
 WQ_BUFS = 5
 T_FIRST = 3
@@ -81,14 +81,13 @@ def tile_neuroplasticitylayer_kernel(
         sq = const.tile([P, NSQ], F32, name="sq")
         tot = const.tile([P, 1], F32, name="tot")
         early = const.tile([P, 1], F32, name="early")
-        nrm = const.tile([P, 1], F32, name="nrm")
         inv = const.tile([P, 1], F32, name="inv")
 
-        nc.vector.memset(brow[:, 0:ROW].bitcast(I32), 0)
         nc.vector.memset(ones_bf[:], 1.0)
         nc.vector.memset(ones_f[:], 1.0)
+        nc.vector.memset(brow[:, 0:ROW].bitcast(I32), 0)
         make_identity(nc, ident[:])
-        nc.scalar.activation(out=warm[:], in_=ones_f[:, 0:1], func=ACT.Sqrt)
+        nc.scalar.activation(out=warm[:], in_=ones_f[:, 0:1], func=ACT.Abs_reciprocal_sqrt)
 
         blocks = []
         c0 = 0
@@ -117,9 +116,9 @@ def tile_neuroplasticitylayer_kernel(
                 nc.sync.dma_start(out=w_sb[w][:, ts, :], in_=w_v[w][:, ts, :])
 
         load_x(0)
-        nc.scalar.dma_start(out=brow[0:1, 0:H], in_=fixed_b.unsqueeze(0))
-        nc.scalar.dma_start(out=brow[0:1, H : H + 1], in_=plasticity_rate.unsqueeze(0))
-        nc.scalar.dma_start(out=brow[0:1, H + 16 : H + 17], in_=hebbian_strength.unsqueeze(0))
+        nc.sync.dma_start(out=brow[0:1, 0:H], in_=fixed_b.unsqueeze(0))
+        nc.sync.dma_start(out=brow[0:1, H : H + 1], in_=plasticity_rate.unsqueeze(0))
+        nc.sync.dma_start(out=brow[0:1, H + 16 : H + 17], in_=hebbian_strength.unsqueeze(0))
         load_x(1)
         load_w(0)
         load_w(1)
@@ -127,11 +126,14 @@ def tile_neuroplasticitylayer_kernel(
             load_w(n)
 
         def bias_everywhere():
-            for i in range(4):
-                bb = next_h([P, ROW // 4])
-                cs = slice(i * ROW // 4, (i + 1) * ROW // 4)
-                nc.tensor.matmul(out=bb[:], lhsT=ones_bf[:, 0:P], rhs=brow[:, cs], start=True, stop=True)
-                nc.scalar.copy(out=bias_bc[:, cs], in_=bb[:])
+            for k, (lo, hi) in enumerate(((0, 1024), (1024, ROW))):
+                bb = psum.tile([P, hi - lo], BF16, name="a_t", tag="A%d" % k)
+                for c in range(lo, hi, 512):
+                    d = min(c + 512, hi)
+                    nc.tensor.matmul(
+                        out=bb[:, c - lo : d - lo], lhsT=ones_bf[:, 0:P], rhs=brow[:, c:d], start=True, stop=True
+                    )
+                nc.scalar.copy(out=bias_bc[:, lo:hi], in_=bb[:])
 
         state = {"h": 0, "sq": 0, "a": 0}
         wcodes = {}
@@ -343,24 +345,25 @@ def tile_neuroplasticitylayer_kernel(
             else:
                 rounds.append((b, (0, 1, 2, 3)))
         tq = list(range(NU))
-        warm_up(5)
+        warm_up(6)
         drain(t_x(0, (1,)))
-        warm_up(1)
+        bias_everywhere()
         pre_q = []
         qx1 = t_x(1, ())
         warm_up(2)
         pre_q.append(pre_chunk(0))
         drain(qx1)
+        drain(pre_q)
         qw0 = t_w(tq.pop(0))
         warm_up(2)
         pre_q.append(pre_chunk(1))
-        drain(pre_q)
         drain(qw0)
+        drain(pre_q)
         qw1 = t_w(tq.pop(0))
+        warm_up(2)
+        drain(qw1)
         pre_q.append(pre_chunk(2))
         drain(pre_q)
-        drain(qw1)
-        bias_everywhere()
         q_prev = t_w(tq.pop(0))
         for r, (b, js) in enumerate(rounds):
             half = len(js) // 2
@@ -415,10 +418,9 @@ def tile_neuroplasticitylayer_kernel(
         parts = [early[:]] + [sq[:, i : i + 1] for i in range(nearly, nsq)]
         for i, part in enumerate(parts):
             nc.tensor.matmul(out=tp[:], lhsT=ones_f[:], rhs=part, start=(i == 0), stop=(i == len(parts) - 1))
-        nc.vector.tensor_scalar_max(out=tot[:], in0=tp[:], scalar1=1.0)
-        nc.scalar.activation(out=nrm[:], in_=tot[:], func=ACT.Sqrt)
-        nc.vector.reciprocal(out=inv[:], in_=nrm[:])
-        pieces = [(0, 0, 512), (0, 512, H)] + [(it, 0, H) for it in range(1, NT)]
+        nc.scalar.activation(out=tot[:], in_=tp[:], func=ACT.Relu, bias=-1.0)
+        nc.scalar.activation(out=inv[:], in_=tot[:], func=ACT.Abs_reciprocal_sqrt, bias=1.0)
+        pieces = [(0, 0, 512), (0, 512, 1024), (0, 1024, H)] + [(it, 0, H) for it in range(1, NT)]
         for i, (it, lo, hi) in enumerate(pieces):
             if i % 3 == 1:
                 nc.scalar.activation(out=t_sb[:, it, lo:hi], in_=t_sb[:, it, lo:hi], func=ACT.Copy, scale=inv[:, 0:1])

@@ -54,11 +54,10 @@ def tile_neuroplasticitylayer_kernel(
 
         x_v = x.flatten_outer_dims().rearrange("(p j) h -> p j h", j=NJ)
         out0_v = out_0.flatten_outer_dims().rearrange("(p j) o -> p j o", j=NJ)
-        w_v = [
-            plastic_weights.rearrange("(t p) h -> p t h", p=P),
-            fixed_w.rearrange("(t p) h -> p t h", p=P),
-        ]
-        out1_v = out_1.rearrange("(t p) o -> p t o", p=P)
+        weights = [plastic_weights, fixed_w]
+
+        def rows_of(dram, c0, wd):
+            return dram[c0 : c0 + wd, :].rearrange("(p a) h -> p a h", a=wd // P)
 
         x_sb = big.tile([P, NJ, H], BF16, name="x_sb")
         pw_sb = big.tile([P, NT, H], BF16, name="pw_sb")
@@ -84,8 +83,8 @@ def tile_neuroplasticitylayer_kernel(
         inv = const.tile([P, 1], F32, name="inv")
 
         nc.vector.memset(ones_bf[:], 1.0)
-        nc.vector.memset(ones_f[:], 1.0)
         nc.vector.memset(brow[:, 0:ROW].bitcast(I32), 0)
+        nc.vector.memset(ones_f[:], 1.0)
         make_identity(nc, ident[:])
         nc.scalar.activation(out=warm[:], in_=ones_f[:, 0:1], func=ACT.Abs_reciprocal_sqrt)
 
@@ -113,7 +112,7 @@ def tile_neuroplasticitylayer_kernel(
             c0, wd = blocks[b]
             ts = slice(c0 // P, (c0 + wd) // P)
             for w in ws_:
-                nc.sync.dma_start(out=w_sb[w][:, ts, :], in_=w_v[w][:, ts, :])
+                nc.sync.dma_start(out=w_sb[w][:, ts, :], in_=rows_of(weights[w], c0, wd))
 
         load_x(0)
         nc.sync.dma_start(out=brow[0:1, 0:H], in_=fixed_b.unsqueeze(0))
@@ -203,12 +202,17 @@ def tile_neuroplasticitylayer_kernel(
         def pre_chunk(c):
             g_t = grp.tile([P, 1024], BF16, name="g_t", tag="grp", align_bytes=64)
             cs = slice(c * 256, (c + 1) * 256)
-            pre_dst = g_t[:].rearrange("p (c i t) -> p c t i", i=4, t=4)
-            pre_src = x_sb[:, :, cs].rearrange("p t (c i) -> p c t i", i=4)
             if c in PRE_ON_SCALAR:
-                nc.scalar.copy(out=pre_dst, in_=pre_src)
+                nc.scalar.copy(
+                    out=g_t[:].rearrange("p (c i t) -> p c t i", i=4, t=4),
+                    in_=x_sb[:, :, cs].rearrange("p t (c i) -> p c t i", i=4),
+                )
             else:
-                nc.vector.tensor_copy(out=pre_dst, in_=pre_src)
+                for a in range(2):
+                    nc.vector.tensor_copy(
+                        out=g_t[:, a * 512 : (a + 1) * 512].rearrange("p (c i t) -> p c t i", i=4, t=4),
+                        in_=x_sb[:, :, cs].rearrange("p t (c i a) -> p a c t i", i=4, a=2)[:, a],
+                    )
             return lambda: nc.vector.quantize_mx(out=prec[:, cs].bitcast(FP8X4), scales=pres[:, cs], in_=g_t[:])
 
         def s1(b, j, a_t):
@@ -232,10 +236,14 @@ def tile_neuroplasticitylayer_kernel(
             c0, wd = blocks[b]
             if b not in combs:
                 combs[b] = cb.tile([P, NJ, wd], F32, name="comb", tag="comb")
+            a = wd // P
             nc.vector.tensor_tensor(
-                out=combs[b][:, js[0] : js[-1] + 1, :],
-                in0=a_t[:],
-                in1=bias_bc[:, c0 : c0 + wd].unsqueeze(1).to_broadcast([P, len(js), wd]),
+                out=combs[b][:, js[0] : js[-1] + 1, :].rearrange("p j (r a) -> p j r a", a=a),
+                in0=a_t[:].rearrange("p j (a r) -> p j r a", a=a),
+                in1=bias_bc[:, c0 : c0 + wd]
+                .rearrange("p (r a) -> p r a", a=a)
+                .unsqueeze(1)
+                .to_broadcast([P, len(js), P, a]),
                 op=ALU.add,
             )
 
@@ -420,10 +428,19 @@ def tile_neuroplasticitylayer_kernel(
             nc.tensor.matmul(out=tp[:], lhsT=ones_f[:], rhs=part, start=(i == 0), stop=(i == len(parts) - 1))
         nc.scalar.activation(out=tot[:], in_=tp[:], func=ACT.Relu, bias=-1.0)
         nc.scalar.activation(out=inv[:], in_=tot[:], func=ACT.Abs_reciprocal_sqrt, bias=1.0)
-        pieces = [(0, 0, 512), (0, 512, 1024), (0, 1024, H)] + [(it, 0, H) for it in range(1, NT)]
-        for i, (it, lo, hi) in enumerate(pieces):
-            if i % 3 == 1:
-                nc.scalar.activation(out=t_sb[:, it, lo:hi], in_=t_sb[:, it, lo:hi], func=ACT.Copy, scale=inv[:, 0:1])
+        def scale(on_vector, it, lo, hi):
+            t_v = t_sb[:, it, lo:hi]
+            if on_vector:
+                nc.vector.tensor_scalar_mul(out=t_v, in0=t_v, scalar1=inv[:, 0:1])
             else:
-                nc.vector.tensor_scalar_mul(out=t_sb[:, it, lo:hi], in0=t_sb[:, it, lo:hi], scalar1=inv[:, 0:1])
-            nc.sync.dma_start(out=out1_v[:, it, lo:hi], in_=t_sb[:, it, lo:hi])
+                nc.scalar.activation(out=t_v, in_=t_v, func=ACT.Copy, scale=inv[:, 0:1])
+
+        for it in (NT - 2, NT - 1):
+            for i in range(3):
+                cs = slice(i * 512, (i + 1) * 512)
+                scale(i != 1, it, cs.start, cs.stop)
+                nc.sync.dma_start(out=out_1[it * P : (it + 1) * P, cs], in_=t_sb[:, it, cs])
+        for it in range(0, NT - 2, 2):
+            scale(False, it, 0, H)
+            scale(True, it + 1, 0, H)
+            nc.sync.dma_start(out=rows_of(out_1, it * P, 2 * P), in_=t_sb[:, it : it + 2, :])

@@ -150,7 +150,7 @@ def tile_neuroplasticitylayer_kernel(
             return psum.tile(shape, F32, name="hb", tag="H%d" % i)
 
         def warm_up(n):
-            junk = psum.tile([P, 512], F32, name="a_t", tag="A1")
+            junk = psum.tile([P, 512], F32, name="a_t", tag="A0")
             for i in range(n):
                 nc.tensor.matmul(out=junk[:], lhsT=ones_bf[:, 0:P], rhs=ones_bf[:], start=True, stop=True)
 
@@ -375,7 +375,7 @@ def tile_neuroplasticitylayer_kernel(
         q_prev = t_w(tq.pop(0))
         for r, (b, js) in enumerate(rounds):
             half = len(js) // 2
-            jobs = s2_run(S2_PER_ROUND)
+            jobs = s2_run(S2_PER_ROUND if r < len(rounds) - 1 else NH)
             a_t = psum.tile([P, len(js), blocks[b][1]], F32, name="a_t", tag="A%d" % (r % 2))
             for j in js[:half]:
                 s1(b, j, a_t[:, j - js[0], :])
@@ -385,11 +385,11 @@ def tile_neuroplasticitylayer_kernel(
                 s1(b, j, a_t[:, j - js[0], :])
             drain(q_prev)
             q_prev = q_next
-            drain(pre_q)
             drain(v_later)
             for job in jobs:
                 s2_out(*job)
             drain(post_q)
+            drain(pre_q)
             v_later.append(lambda b=b, js=js, a_t=a_t: close_rows(b, js, a_t))
             if r == 0:
                 nc.vector.scalar_tensor_tensor(
@@ -435,12 +435,11 @@ def tile_neuroplasticitylayer_kernel(
             else:
                 nc.scalar.activation(out=t_v, in_=t_v, func=ACT.Copy, scale=inv[:, 0:1])
 
-        for it in (NT - 2, NT - 1):
-            for i in range(3):
-                cs = slice(i * 512, (i + 1) * 512)
-                scale(i != 1, it, cs.start, cs.stop)
-                nc.sync.dma_start(out=out_1[it * P : (it + 1) * P, cs], in_=t_sb[:, it, cs])
-        for it in range(0, NT - 2, 2):
-            scale(False, it, 0, H)
+        plain = NT - 2
+        for on_vector, it, lo, hi in ((True, plain, 0, 512), (True, plain, 512, H), (False, plain + 1, 0, H)):
+            scale(on_vector, it, lo, hi)
+            nc.sync.dma_start(out=out_1[it * P : (it + 1) * P, lo:hi], in_=t_sb[:, it, lo:hi])
+        for it in range(0, plain, 2):
+            scale(it == 0, it, 0, H)
             scale(True, it + 1, 0, H)
             nc.sync.dma_start(out=rows_of(out_1, it * P, 2 * P), in_=t_sb[:, it : it + 2, :])

@@ -256,6 +256,10 @@ def tile_neuroplasticitylayer_kernel(
                 nc.vector.tensor_copy(
                     out=cg[:].rearrange("p (o j) -> p o j", j=NJ), in_=comb[:].rearrange("p j o -> p o j")
                 )
+            elif b in (5,):
+                nc.scalar.copy(
+                    out=cg[:].rearrange("p (o j) -> p o j", j=NJ), in_=comb[:].rearrange("p j o -> p o j")
+                )
             else:
                 nc.gpsimd.tensor_scalar(
                     out=cg[:].rearrange("p (o j) -> p o j", j=NJ),
@@ -357,17 +361,17 @@ def tile_neuroplasticitylayer_kernel(
         drain(t_x(0, (1,)))
         bias_everywhere()
         pre_q = []
-        qx1 = t_x(1, ())
-        warm_up(2)
         pre_q.append(pre_chunk(0))
+        qx1 = t_x(1, (1,))
+        warm_up(2)
         drain(qx1)
         drain(pre_q)
-        qw0 = t_w(tq.pop(0))
+        qw0 = t_w(tq.pop(0), ())
         warm_up(2)
         pre_q.append(pre_chunk(1))
         drain(qw0)
         drain(pre_q)
-        qw1 = t_w(tq.pop(0))
+        qw1 = t_w(tq.pop(0), ())
         warm_up(2)
         drain(qw1)
         pre_q.append(pre_chunk(2))

@@ -446,4 +446,5 @@ def tile_neuroplasticitylayer_kernel(
         for it in range(0, plain, 2):
             scale(it == 0, it, 0, H)
             scale(True, it + 1, 0, H)
-            nc.sync.dma_start(out=rows_of(out_1, it * P, 2 * P), in_=t_sb[:, it : it + 2, :])
+            queue = nc.scalar if it % 4 == 2 else nc.sync
+            queue.dma_start(out=rows_of(out_1, it * P, 2 * P), in_=t_sb[:, it : it + 2, :])

from contextlib import ExitStack

import concourse.bass as bass
import concourse.mybir as mybir
import concourse.tile as tile
from concourse.masks import make_identity

F32 = mybir.dt.float32
BF16 = mybir.dt.bfloat16
U32 = mybir.dt.uint32
U8 = mybir.dt.uint8
I32 = mybir.dt.int32
FP8X4 = mybir.dt.float8_e4m3fn_x4
ALU = mybir.AluOpType
ACT = mybir.ActivationFunctionType
AX = mybir.AxisListType

P = 128
H = 1536
M = 512
KP = 512
NG = H // KP
NJ = M // P
BW = 256
NB = H // BW
NT = H // P
FLOPS = 3 * 2 * M * H * H
PINNED = True
S2_PER_ROUND = 3
WIDTHS = (256, 256, 256, 256, 256, 128, 128)
FAST = (0, 6)
NH = 6
ROW = H + 32
LAST_ON_VECTOR = ()
PRE_ON_SCALAR = (5,)
WQ_BUFS = 5
T_FIRST = 3
T_PER_ROUND = (1, 1, 1, 1, 1, 1, 1, 1, 1, 1)


def tile_neuroplasticitylayer_kernel(
    tc, x, plastic_weights, plasticity_rate, fixed_w, fixed_b, hebbian_strength, out_0, out_1
):
    nc = tc.nc
    with ExitStack() as ctx:
        if PINNED:
            ctx.enter_context(tc.manual_schedule())
        const = ctx.enter_context(tc.tile_pool(name="const", bufs=1))
        big = ctx.enter_context(tc.tile_pool(name="big", bufs=1))
        grp = ctx.enter_context(tc.tile_pool(name="grp", bufs=8))
        wq = ctx.enter_context(tc.tile_pool(name="wq", bufs=WQ_BUFS))
        cb = ctx.enter_context(tc.tile_pool(name="cb", bufs=3))
        psum = ctx.enter_context(tc.psum_pool(name="psum", bufs=1))

        x_v = x.flatten_outer_dims().rearrange("(p j) h -> p j h", j=NJ)
        out0_v = out_0.flatten_outer_dims().rearrange("(p j) o -> p j o", j=NJ)
        weights = [plastic_weights, fixed_w]

        def rows_of(dram, c0, wd):
            return dram[c0 : c0 + wd, :].rearrange("(p a) h -> p a h", a=wd // P)

        x_sb = big.tile([P, NJ, H], BF16, name="x_sb")
        pw_sb = big.tile([P, NT, H], BF16, name="pw_sb")
        fw_sb = big.tile([P, NT, H], BF16, name="fw_sb")
        w_sb = [pw_sb, fw_sb]
        t_sb = big.tile([P, NT, H], F32, name="t_sb")
        xc = big.tile([P, NG, M], U32, name="xc", align_bytes=64)
        xs = big.tile([P, NG, M], U8, name="xs", align_bytes=64)
        prec = big.tile([P, H], U32, name="prec", align_bytes=64)
        pres = big.tile([P, H], U8, name="pres", align_bytes=64)

        ident = const.tile([P, P], F32, name="ident")
        ones_bf = const.tile([P, 512], BF16, name="ones_bf")
        ones_f = const.tile([P, P], F32, name="ones_f")
        brow = cb.tile([P, 2048], BF16, name="brow", tag="comb")
        bias_bc = const.tile([P, ROW], BF16, name="bias_bc")
        cfac = const.tile([P, 1], F32, name="cfac")
        warm = const.tile([P, 1], F32, name="warm")
        NSQ = 40
        sq = const.tile([P, NSQ], F32, name="sq")
        tot = const.tile([P, 1], F32, name="tot")
        early = const.tile([P, 1], F32, name="early")
        inv = const.tile([P, 1], F32, name="inv")

        nc.vector.memset(ones_bf[:], 1.0)
        nc.vector.memset(brow[:, 0:ROW].bitcast(I32), 0)
        nc.vector.memset(ones_f[:], 1.0)
        make_identity(nc, ident[:])
        nc.scalar.activation(out=warm[:], in_=ones_f[:, 0:1], func=ACT.Abs_reciprocal_sqrt)

        blocks = []
        c0 = 0
        for wd in WIDTHS:
            blocks.append((c0, wd))
            c0 += wd
        assert c0 == H
        units = []
        for b, (c0, wd) in enumerate(blocks):
            if wd == 256:
                units.append((b, (0,)))
                units.append((b, (1,)))
            else:
                units.append((b, (0, 1)))
        NU = len(units)
        block_units = [[n for n in range(NU) if units[n][0] == b] for b in range(len(blocks))]

        def load_x(h):
            nc.sync.dma_start(out=x_sb[:, 2 * h : 2 * h + 2, :], in_=x_v[:, 2 * h : 2 * h + 2, :])

        def load_w(n):
            b, ws_ = units[n]
            c0, wd = blocks[b]
            ts = slice(c0 // P, (c0 + wd) // P)
            for w in ws_:
                nc.sync.dma_start(out=w_sb[w][:, ts, :], in_=rows_of(weights[w], c0, wd))

        load_x(0)
        nc.sync.dma_start(out=brow[0:1, 0:H], in_=fixed_b.unsqueeze(0))
        nc.sync.dma_start(out=brow[0:1, H : H + 1], in_=plasticity_rate.unsqueeze(0))
        nc.sync.dma_start(out=brow[0:1, H + 16 : H + 17], in_=hebbian_strength.unsqueeze(0))
        load_x(1)
        load_w(0)
        load_w(1)
        for n in range(2, NU):
            load_w(n)

        def bias_everywhere():
            for k, (lo, hi) in enumerate(((0, 1024), (1024, ROW))):
                bb = psum.tile([P, hi - lo], BF16, name="a_t", tag="A%d" % k)
                for c in range(lo, hi, 512):
                    d = min(c + 512, hi)
                    nc.tensor.matmul(
                        out=bb[:, c - lo : d - lo], lhsT=ones_bf[:, 0:P], rhs=brow[:, c:d], start=True, stop=True
                    )
                nc.scalar.copy(out=bias_bc[:, lo:hi], in_=bb[:])

        state = {"h": 0, "sq": 0, "a": 0}
        wcodes = {}
        acc = {}
        posts = {}
        combs = {}
        s2_ready = []
        to_square = []
        v_later = []
        post_q = []

        def next_h(shape):
            i = state["h"] % NH
            state["h"] += 1
            return psum.tile(shape, F32, name="hb", tag="H%d" % i)

        def warm_up(n):
            junk = psum.tile([P, 512], F32, name="a_t", tag="A0")
            for i in range(n):
                nc.tensor.matmul(out=junk[:], lhsT=ones_bf[:, 0:P], rhs=ones_bf[:], start=True, stop=True)

        def transpose_bank(srcs):
            bank = next_h([P, 2, 2, P])
            for i in range(4):
                nc.tensor.transpose(out=bank[:, i // 2, i % 2, :], in_=srcs[i].bitcast(F32), identity=ident[:])
            return bank

        def exit_bank(bank, on_vector):
            g_t = grp.tile([P, 1024], BF16, name="g_t", tag="grp", align_bytes=64)
            dst = g_t[:].bitcast(F32).rearrange("p (a r u) -> p a r u", a=2, u=2)
            src = bank[:].rearrange("p a u r -> p a r u")
            if on_vector:
                nc.vector.tensor_copy(out=dst, in_=src)
            else:
                nc.scalar.copy(out=dst, in_=src)
            return g_t

        def t_rows(rows, codes, planes, on_vector=()):
            banks = [
                transpose_bank([row[:, g * KP + u * 256 : g * KP + (u + 1) * 256] for row in rows for u in range(2)])
                for g in range(NG)
            ]
            tiles = [exit_bank(bank, g in on_vector) for g, bank in enumerate(banks)]
            return [
                lambda g=g: nc.vector.quantize_mx(out=codes[g].bitcast(FP8X4), scales=planes[g], in_=tiles[g][:])
                for g in range(NG)
            ]

        def t_x(h, on_vector):
            hs = slice(h * 256, (h + 1) * 256)
            return t_rows(
                [x_sb[:, 2 * h + a, :] for a in range(2)],
                [xc[:, g, hs] for g in range(NG)],
                [xs[:, g, hs] for g in range(NG)],
                on_vector,
            )

        def t_w(n, on_vector=()):
            b, ws_ = units[n]
            t0 = blocks[b][0] // P
            rows = [w_sb[ws_[0]][:, t0 + a, :] for a in range(2)] if len(ws_) == 1 else [w_sb[w][:, t0, :] for w in ws_]
            wc = wq.tile([P, NG, BW], U32, name="wc", tag="wc", align_bytes=64)
            ws = wq.tile([P, NG, BW], U8, name="ws", tag="ws", align_bytes=64)
            wcodes[n] = (wc, ws)
            return t_rows(rows, [wc[:, g, :] for g in range(NG)], [ws[:, g, :] for g in range(NG)], on_vector)

        def pre_chunk(c):
            g_t = grp.tile([P, 1024], BF16, name="g_t", tag="grp", align_bytes=64)
            cs = slice(c * 256, (c + 1) * 256)
            if c in PRE_ON_SCALAR:
                nc.scalar.copy(
                    out=g_t[:].rearrange("p (c i t) -> p c t i", i=4, t=4),
                    in_=x_sb[:, :, cs].rearrange("p t (c i) -> p c t i", i=4),
                )
            else:
                for a in range(2):
                    nc.vector.tensor_copy(
                        out=g_t[:, a * 512 : (a + 1) * 512].rearrange("p (c i t) -> p c t i", i=4, t=4),
                        in_=x_sb[:, :, cs].rearrange("p t (c i a) -> p a c t i", i=4, a=2)[:, a],
                    )
            return lambda: nc.vector.quantize_mx(out=prec[:, cs].bitcast(FP8X4), scales=pres[:, cs], in_=g_t[:])

        def s1(b, j, a_t):
            c0, wd = blocks[b]
            sl = slice(j * P, (j + 1) * P)
            passes = [(n, w, g) for n in block_units[b] for w in units[n][1] for g in range(NG)]
            for i, (n, w, g) in enumerate(passes):
                wc, ws = wcodes[n]
                cs = slice(0, wd) if len(units[n][1]) == 1 else slice(w * wd, (w + 1) * wd)
                nc.tensor.matmul_mx(
                    out=a_t,
                    lhsT=xc[:, g, sl].bitcast(FP8X4),
                    lhsT_scale=xs[:, g, sl],
                    rhs=wc[:, g, cs].bitcast(FP8X4),
                    rhs_scale=ws[:, g, cs],
                    start=(i == 0),
                    stop=(i == len(passes) - 1),
                )

        def close_rows(b, js, a_t):
            c0, wd = blocks[b]
            if b not in combs:
                combs[b] = cb.tile([P, NJ, wd], F32, name="comb", tag="comb")
            a = wd // P
            nc.vector.tensor_tensor(
                out=combs[b][:, js[0] : js[-1] + 1, :].rearrange("p j (r a) -> p j r a", a=a),
                in0=a_t[:].rearrange("p j (a r) -> p j r a", a=a),
                in1=bias_bc[:, c0 : c0 + wd]
                .rearrange("p (r a) -> p r a", a=a)
                .unsqueeze(1)
                .to_broadcast([P, len(js), P, a]),
                op=ALU.add,
            )

        def close_block(b, fast):
            c0, wd = blocks[b]
            comb = combs[b]
            nc.sync.dma_start(out=out0_v[:, :, c0 : c0 + wd], in_=comb[:])
            cg = cb.tile([P, wd * NJ], BF16, name="cg", tag="cg", align_bytes=64)
            if fast:
                nc.vector.tensor_copy(
                    out=cg[:].rearrange("p (o j) -> p o j", j=NJ), in_=comb[:].rearrange("p j o -> p o j")
                )
            elif b in (5,):
                nc.scalar.copy(
                    out=cg[:].rearrange("p (o j) -> p o j", j=NJ), in_=comb[:].rearrange("p j o -> p o j")
                )
            else:
                nc.gpsimd.tensor_scalar(
                    out=cg[:].rearrange("p (o j) -> p o j", j=NJ),
                    in0=comb[:].rearrange("p j o -> p o j"),
                    scalar1=1.0,
                    scalar2=0.0,
                    op0=ALU.mult,
                    op1=ALU.add,
                )

            def quant():
                pc = cb.tile([P, wd], U32, name="pc", tag="pc", align_bytes=64)
                ps = cb.tile([P, wd], U8, name="ps", tag="ps", align_bytes=64)
                nc.vector.quantize_mx(out=pc[:].bitcast(FP8X4), scales=ps[:], in_=cg[:])
                posts[b] = (pc, ps)
                per = 512 // wd
                for k in range(NT // per):
                    s2_ready.append((b, k * per, per))

            return quant

        def s2_pe(b, t0, per):
            pc, ps = posts[b]
            hb = next_h([P, per, blocks[b][1]])
            for i in range(per):
                ts = slice((t0 + i) * P, (t0 + i + 1) * P)
                nc.tensor.matmul_mx(
                    out=hb[:, i, :],
                    lhsT=prec[:, ts].bitcast(FP8X4),
                    lhsT_scale=pres[:, ts],
                    rhs=pc[:].bitcast(FP8X4),
                    rhs_scale=ps[:],
                    start=True,
                    stop=True,
                )
            return hb

        def s2_out(b, t0, per, hb):
            c0, wd = blocks[b]
            nc.vector.scalar_tensor_tensor(
                out=t_sb[:, t0 : t0 + per, c0 : c0 + wd],
                in0=hb[:],
                scalar=cfac[:, 0:1],
                in1=pw_sb[:, t0 : t0 + per, c0 : c0 + wd],
                op0=ALU.mult,
                op1=ALU.add,
            )
            to_square.append((b, t0, per))

        def squares(group, on_vector=False):
            while to_square:
                b, t0, per = to_square.pop(0)
                n = per
                while n < group * per and to_square and to_square[0] == (b, t0 + n, per):
                    to_square.pop(0)
                    n += per
                c0, wd = blocks[b]
                i = state["sq"]
                state["sq"] += 1
                if on_vector:
                    t_v = t_sb[:, t0 : t0 + n, c0 : c0 + wd]
                    nc.vector.scalar_tensor_tensor(
                        out=fw_sb[:, 0:2, :].bitcast(F32)[:, 0, 0 : n * wd].rearrange("p (a o) -> p a o", o=wd),
                        in0=t_v,
                        scalar=1.0,
                        in1=t_v,
                        op0=ALU.mult,
                        op1=ALU.mult,
                        accum_out=sq[:, i : i + 1],
                    )
                    continue
                nc.scalar.activation(
                    out=x_sb[:, i % 2, 0 : n * wd].rearrange("p (a o) -> p a o", o=wd),
                    in_=t_sb[:, t0 : t0 + n, c0 : c0 + wd],
                    func=ACT.Square,
                    accum_out=sq[:, i : i + 1],
                )

        def s2_run(count):
            jobs = []
            for i in range(min(count, len(s2_ready))):
                job = s2_ready.pop(0)
                jobs.append(job + (s2_pe(*job),))
            return jobs

        def drain(queue):
            while queue:
                queue.pop(0)()

        rounds = []
        for b, (c0, wd) in enumerate(blocks):
            if wd == 256:
                rounds.append((b, (0, 1)))
                rounds.append((b, (2, 3)))
            else:
                rounds.append((b, (0, 1, 2, 3)))
        tq = list(range(NU))
        warm_up(6)
        drain(t_x(0, (1,)))
        bias_everywhere()
        pre_q = []
        pre_q.append(pre_chunk(0))
        qx1 = t_x(1, (1,))
        warm_up(2)
        drain(qx1)
        drain(pre_q)
        qw0 = t_w(tq.pop(0), ())
        warm_up(2)
        pre_q.append(pre_chunk(1))
        drain(qw0)
        drain(pre_q)
        qw1 = t_w(tq.pop(0), ())
        warm_up(2)
        drain(qw1)
        pre_q.append(pre_chunk(2))
        drain(pre_q)
        q_prev = t_w(tq.pop(0))
        for r, (b, js) in enumerate(rounds):
            half = len(js) // 2
            jobs = s2_run(S2_PER_ROUND if r < len(rounds) - 1 else NH)
            a_t = psum.tile([P, len(js), blocks[b][1]], F32, name="a_t", tag="A%d" % (r % 2))
            for j in js[:half]:
                s1(b, j, a_t[:, j - js[0], :])
            squares(3)
            q_next = t_w(tq.pop(0)) if tq else []
            for j in js[half:]:
                s1(b, j, a_t[:, j - js[0], :])
            drain(q_prev)
            q_prev = q_next
            drain(v_later)
            for job in jobs:
                s2_out(*job)
            drain(post_q)
            drain(pre_q)
            v_later.append(lambda b=b, js=js, a_t=a_t: close_rows(b, js, a_t))
            if r == 0:
                nc.vector.scalar_tensor_tensor(
                    out=cfac[:],
                    in0=bias_bc[:, H : H + 1],
                    scalar=1.0 / M,
                    in1=bias_bc[:, H + 16 : H + 17],
                    op0=ALU.mult, op1=ALU.mult
                )
            if r < 3:
                pre_q.append(pre_chunk(3 + r))
            if js[-1] == NJ - 1:
                v_later.append(lambda b=b: post_q.append(close_block(b, b in FAST)))
        nearly = state["sq"]
        backlog = s2_run(len(s2_ready))
        squares(3)
        drain(v_later)
        nc.vector.tensor_reduce(out=early[:], in_=sq[:, 0:nearly], axis=AX.X, op=ALU.add)
        for job in backlog[:1]:
            s2_out(*job)
        squares(1)
        drain(post_q)
        for job in backlog[1:]:
            s2_out(*job)
            squares(1)
        while s2_ready:
            for job in s2_run(1):
                s2_out(*job)
            squares(1, on_vector=len(s2_ready) in LAST_ON_VECTOR)

        nsq = state["sq"]
        assert nsq <= NSQ
        tp = psum.tile([P, 1], F32, name="tp", tag="A0")
        parts = [early[:]] + [sq[:, i : i + 1] for i in range(nearly, nsq)]
        for i, part in enumerate(parts):
            nc.tensor.matmul(out=tp[:], lhsT=ones_f[:], rhs=part, start=(i == 0), stop=(i == len(parts) - 1))
        nc.scalar.activation(out=tot[:], in_=tp[:], func=ACT.Relu, bias=-1.0)
        nc.scalar.activation(out=inv[:], in_=tot[:], func=ACT.Abs_reciprocal_sqrt, bias=1.0)
        def scale(on_vector, it, lo, hi):
            t_v = t_sb[:, it, lo:hi]
            if on_vector:
                nc.vector.tensor_scalar_mul(out=t_v, in0=t_v, scalar1=inv[:, 0:1])
            else:
                nc.scalar.activation(out=t_v, in_=t_v, func=ACT.Copy, scale=inv[:, 0:1])

        plain = NT - 2
        for on_vector, it, lo, hi in ((True, plain, 0, 512), (True, plain, 512, H), (False, plain + 1, 0, H)):
            scale(on_vector, it, lo, hi)
            nc.sync.dma_start(out=out_1[it * P : (it + 1) * P, lo:hi], in_=t_sb[:, it, lo:hi])
        for it in range(0, plain, 2):
            scale(it == 0, it, 0, H)
            scale(True, it + 1, 0, H)
            queue = nc.scalar if it % 4 == 2 else nc.sync
            queue.dma_start(out=rows_of(out_1, it * P, 2 * P), in_=t_sb[:, it : it + 2, :])
